import numpy as np
import ml_dtypes


def mxq(x, axis, fmt="e4m3"):
    dtype, down = {"e4m3": (ml_dtypes.float8_e4m3fn, 7), "e5m2": (ml_dtypes.float8_e5m2, 14)}[fmt]
    v = np.moveaxis(np.asarray(x, np.float32).astype(ml_dtypes.bfloat16).astype(np.float64), axis, -1)
    blocks = v.reshape(v.shape[:-1] + (-1, 32))
    amax = np.abs(blocks).max(-1, keepdims=True)
    byte = np.maximum(np.where(amax > 0, np.frexp(amax)[1] - 1 + 127, 0) - down, 1)
    scale = np.exp2(byte - 127.0)
    codes = (blocks / scale).astype(np.float32).astype(dtype).astype(np.float64)
    return np.moveaxis((codes * scale).reshape(v.shape), -1, axis)


WIDE = False


def mx_kscale(k):
    if not WIDE:
        return np.ones(k)
    levels = np.array([10, -10, 5, -5, 0])
    if k % 512:
        return np.exp2(np.random.permutation(np.resize(levels, k // 32))).repeat(32)
    a = np.empty((k // 512, 16))
    for p in range(k // 512):
        a[p, :8] = np.random.permutation(np.resize(levels, 8))
        for g in range(8):
            far = levels[np.abs(levels - a[p, g]) >= 10]
            a[p, g + 8] = far[np.random.randint(len(far))]
    return np.exp2(a.ravel()).repeat(32)


BF16 = ml_dtypes.bfloat16


def bf(x):
    return np.asarray(x, np.float32).astype(BF16)


def f64(x):
    return np.asarray(x).astype(np.float64)


B, L, D, H = 1, 4096, 512, 2


def setup_inputs():
    s = mx_kscale(D)
    return {"x": bf(np.random.standard_normal((B, L, D)) * s),
            "w": bf(np.random.standard_normal((H, D, D)) / np.sqrt(D) / s[:, None] * s[None, :])}


def reference(x, w):
    wq = mxq(f64(w), 1, "e4m3")
    xq = mxq(f64(x), 2, "e4m3")
    xs = (xq[None] @ wq[:, None]).reshape(H * B, L, D)
    return mxq(xs, 2, "e4m3") @ wq

@@ -1,0 +1,202 @@
+from contextlib import ExitStack
+
+import concourse.mybir as mybir
+from concourse.masks import make_identity
+
+BF16 = mybir.dt.bfloat16
+F32 = mybir.dt.float32
+U32 = mybir.dt.uint32
+U8 = mybir.dt.uint8
+FP8X4 = mybir.dt.float8_e4m3fn_x4
+
+P = 128
+PACK = 4
+PSUM_BANKS = 8
+PAIRS = 2
+L, D, H = 4096, 512, 2
+BLOCKS = 2
+CHUNK = P * BLOCKS
+CHUNKS = L // CHUNK
+STEPS = CHUNKS * H
+LAG = 3
+ROUND = 5
+VECTOR_TURNS = (0, 2)
+
+FLOPS = 2 * H * 2 * L * D * D
+
+
+def tile_multiheadattention_pa_t_kernel(tc, x, w, out):
+    nc = tc.nc
+    x_chunks = x[0].rearrange("(c p j) k -> c p (j k)", p=P, j=BLOCKS)
+    out_chunks = out.rearrange("h (c p j) n -> h c p (j n)", p=P, j=BLOCKS)
+
+    with ExitStack() as ctx:
+        keep = ctx.enter_context(tc.tile_pool(name="keep", bufs=1))
+        x_pool = ctx.enter_context(tc.tile_pool(name="x_rows", bufs=CHUNKS))
+        x_stage = ctx.enter_context(tc.tile_pool(name="x_stage", bufs=2))
+        xs_stage = ctx.enter_context(tc.tile_pool(name="xs_stage", bufs=LAG + 1))
+        out_stage = ctx.enter_context(tc.tile_pool(name="out_stage", bufs=6))
+        banks = ctx.enter_context(tc.psum_pool(name="banks", bufs=PSUM_BANKS))
+
+        emptied = []
+
+        def empty_bank(dst, bank):
+            turn = len(emptied) % ROUND
+            emptied.append(turn)
+            if turn in VECTOR_TURNS:
+                nc.vector.tensor_copy(out=dst, in_=bank)
+            else:
+                nc.scalar.copy(out=dst, in_=bank)
+
+        x_rows = []
+        w_rows = []
+
+        def load_x(c):
+            rows = x_pool.tile([P, BLOCKS * D], BF16, tag="x_rows")
+            nc.sync.dma_start(out=rows[:], in_=x_chunks[c])
+            x_rows.append(rows)
+
+        def load_w(h):
+            rows = keep.tile([P, PACK, D], BF16, tag="w_rows%d" % h)
+            nc.sync.dma_start(
+                out=rows[:].rearrange("p t n -> p (t n)"),
+                in_=w[h].rearrange("(p t) n -> p (t n)", t=PACK),
+            )
+            w_rows.append(rows)
+
+        load_w(0)
+        load_x(0)
+        load_w(1)
+        for c in range(1, CHUNKS):
+            load_x(c)
+
+        identity = keep.tile([P, P], F32)
+        make_identity(nc, identity[:])
+
+        w_codes = keep.tile([P, H, D], U32, align_bytes=64)
+        w_scales = keep.tile([P, H, D], U8, align_bytes=64)
+        w_grouped = []
+
+        def group_w(h, copy):
+            grouped = keep.tile([P, D * PACK], BF16, tag="w_grouped%d" % h, align_bytes=64)
+            copy(
+                out=grouped[:].rearrange("p (t m k) -> p t m k", t=PACK, k=PACK),
+                in_=w_rows[h][:].rearrange("p k (m t) -> p t m k", t=PACK),
+            )
+            w_grouped.append(grouped)
+
+        def quantise_w(h):
+            nc.vector.quantize_mx(
+                out=w_codes[:, h, :].bitcast(FP8X4), scales=w_scales[:, h, :], in_=w_grouped[h][:]
+            )
+
+        x_grouped = {}
+        x_codes = {}
+        x_scales = {}
+
+        def transpose_x(c):
+            words = x_rows[c][:].bitcast(F32)
+            grouped = x_stage.tile([P, CHUNK * PACK], BF16, tag="x_grouped", align_bytes=64)
+            xt = banks.tile([P, PAIRS, CHUNK], F32, tag="bank")
+            for j in range(BLOCKS):
+                row = words[:, j * P * PAIRS : (j + 1) * P * PAIRS]
+                for u in range(PAIRS):
+                    nc.tensor.transpose(xt[:, u, j * P : (j + 1) * P], row[:, u::PAIRS], identity[:])
+            empty_bank(
+                grouped[:].bitcast(F32).rearrange("p (r u) -> p r u", u=PAIRS),
+                xt[:].rearrange("p u r -> p r u"),
+            )
+            x_grouped[c] = grouped
+
+        def quantise_x(c):
+            codes = x_stage.tile([P, CHUNK], U32, tag="x_codes", align_bytes=64)
+            scales = x_stage.tile([P, CHUNK], U8, tag="x_scales", align_bytes=64)
+            nc.vector.quantize_mx(out=codes[:].bitcast(FP8X4), scales=scales[:], in_=x_grouped[c][:])
+            x_codes[c] = codes
+            x_scales[c] = scales
+
+        xs_grouped = {}
+        xs_codes = {}
+        xs_scales = {}
+
+        def first_product(s, j):
+            c, h = divmod(s, H)
+            if j == 0:
+                grouped = xs_stage.tile([P, CHUNK * PACK], BF16, tag="xs_grouped", align_bytes=64)
+                xs_grouped[s] = grouped
+            rows = slice(j * P, (j + 1) * P)
+            xs_t = banks.tile([P, PACK, P], F32, tag="bank")
+            for t in range(PACK):
+                cols = slice(t * P, (t + 1) * P)
+                nc.tensor.matmul_mx(
+                    out=xs_t[:, t, :],
+                    lhsT=w_codes[:, h, cols].bitcast(FP8X4),
+                    lhsT_scale=w_scales[:, h, cols],
+                    rhs=x_codes[c][:, rows].bitcast(FP8X4),
+                    rhs_scale=x_scales[c][:, rows],
+                    start=True,
+                    stop=True,
+                )
+            empty_bank(
+                xs_grouped[s][:, j * P * PACK : (j + 1) * P * PACK].rearrange(
+                    "p (r t) -> p r t", t=PACK
+                ),
+                xs_t[:].rearrange("p t r -> p r t"),
+            )
+
+        def quantise_xs(s):
+            codes = xs_stage.tile([P, CHUNK], U32, tag="xs_codes", align_bytes=64)
+            scales = xs_stage.tile([P, CHUNK], U8, tag="xs_scales", align_bytes=64)
+            nc.vector.quantize_mx(out=codes[:].bitcast(FP8X4), scales=scales[:], in_=xs_grouped[s][:])
+            xs_codes[s] = codes
+            xs_scales[s] = scales
+
+        out_rows = {}
+
+        def second_product(s, j):
+            c, h = divmod(s, H)
+            if j == 0:
+                result = out_stage.tile([P, BLOCKS, D], F32, tag="out_rows")
+                out_rows[s] = result
+            rows = slice(j * P, (j + 1) * P)
+            acc = banks.tile([P, D], F32, tag="bank")
+            nc.tensor.matmul_mx(
+                out=acc[:],
+                lhsT=xs_codes[s][:, rows].bitcast(FP8X4),
+                lhsT_scale=xs_scales[s][:, rows],
+                rhs=w_codes[:, h, :].bitcast(FP8X4),
+                rhs_scale=w_scales[:, h, :],
+                start=True,
+                stop=True,
+            )
+            empty_bank(
+                out_rows[s][:, j, :].rearrange("p (m t) -> p m t", t=PACK),
+                acc[:].rearrange("p (t m) -> p m t", t=PACK),
+            )
+            if j == BLOCKS - 1:
+                nc.sync.dma_start(
+                    out=out_chunks[h, c], in_=out_rows[s][:].rearrange("p j n -> p (j n)")
+                )
+
+        ctx.enter_context(tc.manual_schedule())
+        group_w(0, nc.vector.tensor_copy)
+        transpose_x(0)
+        group_w(1, nc.scalar.copy)
+        quantise_w(0)
+        quantise_x(0)
+        quantise_w(1)
+
+        for s in range(STEPS + LAG):
+            c, h = divmod(s, H)
+            next_chunk = h == 0 and c + 1 < CHUNKS
+            if next_chunk:
+                transpose_x(c + 1)
+            for j in range(BLOCKS):
+                if s >= LAG:
+                    second_product(s - LAG, j)
+                if s < STEPS:
+                    first_product(s, j)
+                if j == 0 and 1 <= s <= STEPS:
+                    quantise_xs(s - 1)
+                if j == 1 and next_chunk:
+                    quantise_x(c + 1)

@@ -18,6 +18,8 @@ BLOCKS = 2
 CHUNK = P * BLOCKS
 CHUNKS = L // CHUNK
 STEPS = CHUNKS * H
+RUN = 4
+RUN_STEPS = 2
 LAG = 3
 ROUND = 5
 VECTOR_TURNS = (0, 2)
@@ -33,7 +35,7 @@ def tile_multiheadattention_pa_t_kernel(tc, x, w, out):
     with ExitStack() as ctx:
         keep = ctx.enter_context(tc.tile_pool(name="keep", bufs=1))
         x_pool = ctx.enter_context(tc.tile_pool(name="x_rows", bufs=CHUNKS))
-        x_stage = ctx.enter_context(tc.tile_pool(name="x_stage", bufs=2))
+        x_stage = ctx.enter_context(tc.tile_pool(name="x_stage", bufs=CHUNKS))
         xs_stage = ctx.enter_context(tc.tile_pool(name="xs_stage", bufs=LAG + 1))
         out_stage = ctx.enter_context(tc.tile_pool(name="out_stage", bufs=6))
         banks = ctx.enter_context(tc.psum_pool(name="banks", bufs=PSUM_BANKS))
@@ -186,11 +188,17 @@ def tile_multiheadattention_pa_t_kernel(tc, x, w, out):
         quantise_x(0)
         quantise_w(1)
 
+        transposed = 1
         for s in range(STEPS + LAG):
-            c, h = divmod(s, H)
-            next_chunk = h == 0 and c + 1 < CHUNKS
-            if next_chunk:
-                transpose_x(c + 1)
+            if s == 0:
+                run = 1
+            elif s % RUN_STEPS == 1:
+                run = min(RUN, CHUNKS - transposed)
+            else:
+                run = 0
+            for c in range(transposed, transposed + run):
+                transpose_x(c)
+            transposed += run
             for j in range(BLOCKS):
                 if s >= LAG:
                     second_product(s - LAG, j)
@@ -198,5 +206,5 @@ def tile_multiheadattention_pa_t_kernel(tc, x, w, out):
                     first_product(s, j)
                 if j == 0 and 1 <= s <= STEPS:
                     quantise_xs(s - 1)
-                if j == 1 and next_chunk:
-                    quantise_x(c + 1)
+                if j == 1 and s + 1 < CHUNKS:
+                    quantise_x(s + 1)

@@ -18,8 +18,8 @@ BLOCKS = 2
 CHUNK = P * BLOCKS
 CHUNKS = L // CHUNK
 STEPS = CHUNKS * H
-RUN = 4
-RUN_STEPS = 2
+GROUP = 4
+RUN_STEPS = 4
 LAG = 3
 ROUND = 5
 VECTOR_TURNS = (0, 2)
@@ -42,7 +42,10 @@ def tile_multiheadattention_pa_t_kernel(tc, x, w, out):
 
         emptied = []
 
-        def empty_bank(dst, bank):
+        def empty_bank(dst, bank, copy=None):
+            if copy:
+                copy(out=dst, in_=bank)
+                return
             turn = len(emptied) % ROUND
             emptied.append(turn)
             if turn in VECTOR_TURNS:
@@ -66,10 +69,12 @@ def tile_multiheadattention_pa_t_kernel(tc, x, w, out):
             )
             w_rows.append(rows)
 
-        load_w(0)
         load_x(0)
+        load_w(0)
+        for c in range(1, GROUP):
+            load_x(c)
         load_w(1)
-        for c in range(1, CHUNKS):
+        for c in range(GROUP, CHUNKS):
             load_x(c)
 
         identity = keep.tile([P, P], F32)
@@ -79,24 +84,30 @@ def tile_multiheadattention_pa_t_kernel(tc, x, w, out):
         w_scales = keep.tile([P, H, D], U8, align_bytes=64)
         w_grouped = []
 
-        def group_w(h, copy):
-            grouped = keep.tile([P, D * PACK], BF16, tag="w_grouped%d" % h, align_bytes=64)
-            copy(
-                out=grouped[:].rearrange("p (t m k) -> p t m k", t=PACK, k=PACK),
-                in_=w_rows[h][:].rearrange("p k (m t) -> p t m k", t=PACK),
-            )
+        for h in range(H):
+            grouped = keep.tile([P, PACK, P * PACK], BF16, tag="w_grouped%d" % h, align_bytes=64)
             w_grouped.append(grouped)
 
-        def quantise_w(h):
+        def group_w(h, half, copy):
+            blocks = slice(2 * half, 2 * half + 2)
+            copy(
+                out=w_grouped[h][:, blocks, :].rearrange("p t (m k) -> p t m k", k=PACK),
+                in_=w_rows[h][:].rearrange("p k (m t) -> p t m k", t=PACK)[:, blocks],
+            )
+
+        def quantise_w(h, half):
+            cols = slice(half * D // 2, (half + 1) * D // 2)
             nc.vector.quantize_mx(
-                out=w_codes[:, h, :].bitcast(FP8X4), scales=w_scales[:, h, :], in_=w_grouped[h][:]
+                out=w_codes[:, h, cols].bitcast(FP8X4),
+                scales=w_scales[:, h, cols],
+                in_=w_grouped[h][:, 2 * half : 2 * half + 2, :].rearrange("p t n -> p (t n)"),
             )
 
         x_grouped = {}
         x_codes = {}
         x_scales = {}
 
-        def transpose_x(c):
+        def transpose_x(c, copy=None):
             words = x_rows[c][:].bitcast(F32)
             grouped = x_stage.tile([P, CHUNK * PACK], BF16, tag="x_grouped", align_bytes=64)
             xt = banks.tile([P, PAIRS, CHUNK], F32, tag="bank")
@@ -107,6 +118,7 @@ def tile_multiheadattention_pa_t_kernel(tc, x, w, out):
             empty_bank(
                 grouped[:].bitcast(F32).rearrange("p (r u) -> p r u", u=PAIRS),
                 xt[:].rearrange("p u r -> p r u"),
+                copy,
             )
             x_grouped[c] = grouped
 
@@ -117,12 +129,19 @@ def tile_multiheadattention_pa_t_kernel(tc, x, w, out):
             x_codes[c] = codes
             x_scales[c] = scales
 
+        steps = [
+            (c, h)
+            for first in range(0, CHUNKS, GROUP)
+            for h in range(H)
+            for c in range(first, first + GROUP)
+        ]
+
         xs_grouped = {}
         xs_codes = {}
         xs_scales = {}
 
         def first_product(s, j):
-            c, h = divmod(s, H)
+            c, h = steps[s]
             if j == 0:
                 grouped = xs_stage.tile([P, CHUNK * PACK], BF16, tag="xs_grouped", align_bytes=64)
                 xs_grouped[s] = grouped
@@ -156,7 +175,7 @@ def tile_multiheadattention_pa_t_kernel(tc, x, w, out):
         out_rows = {}
 
         def second_product(s, j):
-            c, h = divmod(s, H)
+            c, h = steps[s]
             if j == 0:
                 result = out_stage.tile([P, BLOCKS, D], F32, tag="out_rows")
                 out_rows[s] = result
@@ -181,24 +200,25 @@ def tile_multiheadattention_pa_t_kernel(tc, x, w, out):
                 )
 
         ctx.enter_context(tc.manual_schedule())
-        group_w(0, nc.vector.tensor_copy)
-        transpose_x(0)
-        group_w(1, nc.scalar.copy)
-        quantise_w(0)
+        transpose_x(0, nc.scalar.copy)
         quantise_x(0)
-        quantise_w(1)
+        group_w(0, 0, nc.vector.tensor_copy)
+        group_w(0, 1, nc.scalar.copy)
+        quantise_w(0, 0)
+        transpose_x(1, nc.scalar.copy)
+        quantise_w(0, 1)
+        quantise_x(1)
 
-        transposed = 1
+        runs = {0: range(2, GROUP)}
+        for g in range(1, CHUNKS // GROUP):
+            runs[2 + (g - 1) * RUN_STEPS] = range(g * GROUP, (g + 1) * GROUP)
+
         for s in range(STEPS + LAG):
-            if s == 0:
-                run = 1
-            elif s % RUN_STEPS == 1:
-                run = min(RUN, CHUNKS - transposed)
-            else:
-                run = 0
-            for c in range(transposed, transposed + run):
+            for c in runs.get(s, ()):
                 transpose_x(c)
-            transposed += run
+            if s == 1:
+                group_w(1, 0, nc.vector.tensor_copy)
+                group_w(1, 1, nc.scalar.copy)
             for j in range(BLOCKS):
                 if s >= LAG:
                     second_product(s - LAG, j)
@@ -206,5 +226,8 @@ def tile_multiheadattention_pa_t_kernel(tc, x, w, out):
                     first_product(s, j)
                 if j == 0 and 1 <= s <= STEPS:
                     quantise_xs(s - 1)
-                if j == 1 and s + 1 < CHUNKS:
-                    quantise_x(s + 1)
+            if s == 2:
+                quantise_w(1, 0)
+                quantise_w(1, 1)
+            if s + 2 < STEPS and steps[s + 2][1] == 0:
+                quantise_x(steps[s + 2][0])

@@ -37,7 +37,7 @@ def tile_multiheadattention_pa_t_kernel(tc, x, w, out):
         x_pool = ctx.enter_context(tc.tile_pool(name="x_rows", bufs=CHUNKS))
         x_stage = ctx.enter_context(tc.tile_pool(name="x_stage", bufs=CHUNKS))
         xs_stage = ctx.enter_context(tc.tile_pool(name="xs_stage", bufs=LAG + 1))
-        out_stage = ctx.enter_context(tc.tile_pool(name="out_stage", bufs=6))
+        out_stage = ctx.enter_context(tc.tile_pool(name="out_stage", bufs=16))
         banks = ctx.enter_context(tc.psum_pool(name="banks", bufs=PSUM_BANKS))
 
         emptied = []

@@ -19,7 +19,7 @@ CHUNK = P * BLOCKS
 CHUNKS = L // CHUNK
 STEPS = CHUNKS * H
 GROUP = 4
-RUN_STEPS = 4
+RUN_STEPS = GROUP * H
 LAG = 3
 ROUND = 5
 VECTOR_TURNS = (0, 2)
@@ -201,9 +201,9 @@ def tile_multiheadattention_pa_t_kernel(tc, x, w, out):
 
         ctx.enter_context(tc.manual_schedule())
         transpose_x(0, nc.scalar.copy)
-        quantise_x(0)
         group_w(0, 0, nc.vector.tensor_copy)
         group_w(0, 1, nc.scalar.copy)
+        quantise_x(0)
         quantise_w(0, 0)
         transpose_x(1, nc.scalar.copy)
         quantise_w(0, 1)

@@ -21,8 +21,8 @@ STEPS = CHUNKS * H
 GROUP = 4
 RUN_STEPS = GROUP * H
 LAG = 3
-ROUND = 5
-VECTOR_TURNS = (0, 2)
+ROUND = 8
+VECTOR_TURNS = (0, 3, 5)
 
 FLOPS = 2 * H * 2 * L * D * D
 

@@ -21,8 +21,9 @@ STEPS = CHUNKS * H
 GROUP = 4
 RUN_STEPS = GROUP * H
 LAG = 3
-ROUND = 8
-VECTOR_TURNS = (0, 3, 5)
+X_TURNS = (4, (2, 3))
+XS_TURNS = (4, (2,))
+OUT_TURNS = (2, (0,))
 
 FLOPS = 2 * H * 2 * L * D * D
 
@@ -36,19 +37,18 @@ def tile_multiheadattention_pa_t_kernel(tc, x, w, out):
         keep = ctx.enter_context(tc.tile_pool(name="keep", bufs=1))
         x_pool = ctx.enter_context(tc.tile_pool(name="x_rows", bufs=CHUNKS))
         x_stage = ctx.enter_context(tc.tile_pool(name="x_stage", bufs=CHUNKS))
-        xs_stage = ctx.enter_context(tc.tile_pool(name="xs_stage", bufs=LAG + 1))
-        out_stage = ctx.enter_context(tc.tile_pool(name="out_stage", bufs=16))
+        x_grouped_pool = ctx.enter_context(tc.tile_pool(name="x_grouped", bufs=6))
+        xs_stage = ctx.enter_context(tc.tile_pool(name="xs_stage", bufs=12))
+        out_stage = ctx.enter_context(tc.tile_pool(name="out_stage", bufs=24))
         banks = ctx.enter_context(tc.psum_pool(name="banks", bufs=PSUM_BANKS))
 
-        emptied = []
+        emptied = {X_TURNS: 0, XS_TURNS: 0, OUT_TURNS: 0}
 
-        def empty_bank(dst, bank, copy=None):
-            if copy:
-                copy(out=dst, in_=bank)
-                return
-            turn = len(emptied) % ROUND
-            emptied.append(turn)
-            if turn in VECTOR_TURNS:
+        def empty_bank(dst, bank, turns):
+            length, vector_turns = turns
+            turn = emptied[turns] % length
+            emptied[turns] += 1
+            if turn in vector_turns:
                 nc.vector.tensor_copy(out=dst, in_=bank)
             else:
                 nc.scalar.copy(out=dst, in_=bank)
@@ -80,6 +80,16 @@ def tile_multiheadattention_pa_t_kernel(tc, x, w, out):
         identity = keep.tile([P, P], F32)
         make_identity(nc, identity[:])
 
+        zeros = keep.tile([P, D], BF16)
+        nc.vector.memset(zeros[:], 0.0)
+        unread = banks.tile([P, D], F32, tag="bank")
+
+        def keep_warm(n):
+            for i in range(n):
+                nc.tensor.matmul(
+                    out=unread[:], lhsT=zeros[:, :P], rhs=zeros[:], start=True, stop=True
+                )
+
         w_codes = keep.tile([P, H, D], U32, align_bytes=64)
         w_scales = keep.tile([P, H, D], U8, align_bytes=64)
         w_grouped = []
@@ -107,9 +117,9 @@ def tile_multiheadattention_pa_t_kernel(tc, x, w, out):
         x_codes = {}
         x_scales = {}
 
-        def transpose_x(c, copy=None):
+        def transpose_x(c):
             words = x_rows[c][:].bitcast(F32)
-            grouped = x_stage.tile([P, CHUNK * PACK], BF16, tag="x_grouped", align_bytes=64)
+            grouped = x_grouped_pool.tile([P, CHUNK * PACK], BF16, tag="x_grouped", align_bytes=64)
             xt = banks.tile([P, PAIRS, CHUNK], F32, tag="bank")
             for j in range(BLOCKS):
                 row = words[:, j * P * PAIRS : (j + 1) * P * PAIRS]
@@ -118,7 +128,7 @@ def tile_multiheadattention_pa_t_kernel(tc, x, w, out):
             empty_bank(
                 grouped[:].bitcast(F32).rearrange("p (r u) -> p r u", u=PAIRS),
                 xt[:].rearrange("p u r -> p r u"),
-                copy,
+                X_TURNS,
             )
             x_grouped[c] = grouped
 
@@ -163,6 +173,7 @@ def tile_multiheadattention_pa_t_kernel(tc, x, w, out):
                     "p (r t) -> p r t", t=PACK
                 ),
                 xs_t[:].rearrange("p t r -> p r t"),
+                XS_TURNS,
             )
 
         def quantise_xs(s):
@@ -193,6 +204,7 @@ def tile_multiheadattention_pa_t_kernel(tc, x, w, out):
             empty_bank(
                 out_rows[s][:, j, :].rearrange("p (m t) -> p m t", t=PACK),
                 acc[:].rearrange("p (t m) -> p m t", t=PACK),
+                OUT_TURNS,
             )
             if j == BLOCKS - 1:
                 nc.sync.dma_start(
@@ -200,12 +212,15 @@ def tile_multiheadattention_pa_t_kernel(tc, x, w, out):
                 )
 
         ctx.enter_context(tc.manual_schedule())
-        transpose_x(0, nc.scalar.copy)
+        keep_warm(4)
+        transpose_x(0)
+        keep_warm(3)
         group_w(0, 0, nc.vector.tensor_copy)
         group_w(0, 1, nc.scalar.copy)
         quantise_x(0)
         quantise_w(0, 0)
-        transpose_x(1, nc.scalar.copy)
+        transpose_x(1)
+        keep_warm(1)
         quantise_w(0, 1)
         quantise_x(1)
 

@@ -20,7 +20,8 @@ CHUNKS = L // CHUNK
 STEPS = CHUNKS * H
 GROUP = 4
 RUN_STEPS = GROUP * H
-LAG = 3
+LAG = 4
+CATCH_UP = STEPS - 4
 X_TURNS = (4, (2, 3))
 XS_TURNS = (4, (2,))
 OUT_TURNS = (2, (0,))
@@ -176,12 +177,17 @@ def tile_multiheadattention_pa_t_kernel(tc, x, w, out):
                 XS_TURNS,
             )
 
-        def quantise_xs(s):
-            codes = xs_stage.tile([P, CHUNK], U32, tag="xs_codes", align_bytes=64)
-            scales = xs_stage.tile([P, CHUNK], U8, tag="xs_scales", align_bytes=64)
-            nc.vector.quantize_mx(out=codes[:].bitcast(FP8X4), scales=scales[:], in_=xs_grouped[s][:])
-            xs_codes[s] = codes
-            xs_scales[s] = scales
+        def quantise_xs(s, rows=slice(0, CHUNK)):
+            if rows.start == 0:
+                codes = xs_stage.tile([P, CHUNK], U32, tag="xs_codes", align_bytes=64)
+                scales = xs_stage.tile([P, CHUNK], U8, tag="xs_scales", align_bytes=64)
+                xs_codes[s] = codes
+                xs_scales[s] = scales
+            nc.vector.quantize_mx(
+                out=xs_codes[s][:, rows].bitcast(FP8X4),
+                scales=xs_scales[s][:, rows],
+                in_=xs_grouped[s][:, rows.start * PACK : rows.stop * PACK],
+            )
 
         out_rows = {}
 
@@ -206,7 +212,12 @@ def tile_multiheadattention_pa_t_kernel(tc, x, w, out):
                 acc[:].rearrange("p (t m) -> p m t", t=PACK),
                 OUT_TURNS,
             )
-            if j == BLOCKS - 1:
+            if s == STEPS - 1:
+                nc.sync.dma_start(
+                    out=out_chunks[h, c].rearrange("p (j n) -> p j n", j=BLOCKS)[:, j, :],
+                    in_=out_rows[s][:, j, :],
+                )
+            elif j == BLOCKS - 1:
                 nc.sync.dma_start(
                     out=out_chunks[h, c], in_=out_rows[s][:].rearrange("p j n -> p (j n)")
                 )
@@ -228,21 +239,29 @@ def tile_multiheadattention_pa_t_kernel(tc, x, w, out):
         for g in range(1, CHUNKS // GROUP):
             runs[2 + (g - 1) * RUN_STEPS] = range(g * GROUP, (g + 1) * GROUP)
 
-        for s in range(STEPS + LAG):
+        done = 0
+        for s in range(STEPS):
             for c in runs.get(s, ()):
                 transpose_x(c)
             if s == 1:
                 group_w(1, 0, nc.vector.tensor_copy)
                 group_w(1, 1, nc.scalar.copy)
+            n = int(s >= LAG) + int(s == CATCH_UP)
+            due = [(q, i) for q in range(done, done + n) for i in range(BLOCKS)]
+            done += n
             for j in range(BLOCKS):
-                if s >= LAG:
-                    second_product(s - LAG, j)
-                if s < STEPS:
-                    first_product(s, j)
-                if j == 0 and 1 <= s <= STEPS:
+                for q, i in due[j * n : (j + 1) * n]:
+                    second_product(q, i)
+                first_product(s, j)
+                if j == 0 and s > 0:
                     quantise_xs(s - 1)
             if s == 2:
                 quantise_w(1, 0)
                 quantise_w(1, 1)
             if s + 2 < STEPS and steps[s + 2][1] == 0:
                 quantise_x(steps[s + 2][0])
+        for q in range(done, STEPS):
+            for i in range(BLOCKS):
+                second_product(q, i)
+                if q == done:
+                    quantise_xs(STEPS - 1, slice(i * P, (i + 1) * P))

@@ -20,6 +20,7 @@ CHUNKS = L // CHUNK
 STEPS = CHUNKS * H
 GROUP = 4
 RUN_STEPS = GROUP * H
+PAIR = 2
 LAG = 4
 CATCH_UP = STEPS - 4
 X_TURNS = (4, (2, 3))
@@ -37,8 +38,8 @@ def tile_multiheadattention_pa_t_kernel(tc, x, w, out):
     with ExitStack() as ctx:
         keep = ctx.enter_context(tc.tile_pool(name="keep", bufs=1))
         x_pool = ctx.enter_context(tc.tile_pool(name="x_rows", bufs=CHUNKS))
-        x_stage = ctx.enter_context(tc.tile_pool(name="x_stage", bufs=CHUNKS))
-        x_grouped_pool = ctx.enter_context(tc.tile_pool(name="x_grouped", bufs=6))
+        x_stage = ctx.enter_context(tc.tile_pool(name="x_stage", bufs=CHUNKS // PAIR))
+        x_grouped_pool = ctx.enter_context(tc.tile_pool(name="x_grouped", bufs=3))
         xs_stage = ctx.enter_context(tc.tile_pool(name="xs_stage", bufs=12))
         out_stage = ctx.enter_context(tc.tile_pool(name="out_stage", bufs=24))
         banks = ctx.enter_context(tc.psum_pool(name="banks", bufs=PSUM_BANKS))
@@ -99,8 +100,17 @@ def tile_multiheadattention_pa_t_kernel(tc, x, w, out):
             grouped = keep.tile([P, PACK, P * PACK], BF16, tag="w_grouped%d" % h, align_bytes=64)
             w_grouped.append(grouped)
 
-        def group_w(h, half, copy):
-            blocks = slice(2 * half, 2 * half + 2)
+        def gpsimd_copy(out, in_):
+            nc.gpsimd.tensor_scalar(
+                out=out,
+                in0=in_,
+                scalar1=1.0,
+                scalar2=0.0,
+                op0=mybir.AluOpType.mult,
+                op1=mybir.AluOpType.add,
+            )
+
+        def group_w(h, blocks, copy):
             copy(
                 out=w_grouped[h][:, blocks, :].rearrange("p t (m k) -> p t m k", k=PACK),
                 in_=w_rows[h][:].rearrange("p k (m t) -> p t m k", t=PACK)[:, blocks],
@@ -120,25 +130,33 @@ def tile_multiheadattention_pa_t_kernel(tc, x, w, out):
 
         def transpose_x(c):
             words = x_rows[c][:].bitcast(F32)
-            grouped = x_grouped_pool.tile([P, CHUNK * PACK], BF16, tag="x_grouped", align_bytes=64)
+            pair, i = divmod(c, PAIR)
+            if i == 0:
+                grouped = x_grouped_pool.tile(
+                    [P, PAIR, CHUNK * PACK], BF16, tag="x_grouped", align_bytes=64
+                )
+                codes = x_stage.tile([P, PAIR, CHUNK], U32, tag="x_codes", align_bytes=64)
+                scales = x_stage.tile([P, PAIR, CHUNK], U8, tag="x_scales", align_bytes=64)
+                x_grouped[pair], x_codes[pair], x_scales[pair] = grouped, codes, scales
             xt = banks.tile([P, PAIRS, CHUNK], F32, tag="bank")
             for j in range(BLOCKS):
                 row = words[:, j * P * PAIRS : (j + 1) * P * PAIRS]
                 for u in range(PAIRS):
                     nc.tensor.transpose(xt[:, u, j * P : (j + 1) * P], row[:, u::PAIRS], identity[:])
             empty_bank(
-                grouped[:].bitcast(F32).rearrange("p (r u) -> p r u", u=PAIRS),
+                x_grouped[pair][:, i, :].bitcast(F32).rearrange("p (r u) -> p r u", u=PAIRS),
                 xt[:].rearrange("p u r -> p r u"),
                 X_TURNS,
             )
-            x_grouped[c] = grouped
 
-        def quantise_x(c):
-            codes = x_stage.tile([P, CHUNK], U32, tag="x_codes", align_bytes=64)
-            scales = x_stage.tile([P, CHUNK], U8, tag="x_scales", align_bytes=64)
-            nc.vector.quantize_mx(out=codes[:].bitcast(FP8X4), scales=scales[:], in_=x_grouped[c][:])
-            x_codes[c] = codes
-            x_scales[c] = scales
+        def quantise_x(first, n):
+            pair, i = divmod(first, PAIR)
+            chunks = slice(i, i + n)
+            nc.vector.quantize_mx(
+                out=x_codes[pair][:, chunks, :].rearrange("p i r -> p (i r)").bitcast(FP8X4),
+                scales=x_scales[pair][:, chunks, :].rearrange("p i r -> p (i r)"),
+                in_=x_grouped[pair][:, chunks, :].rearrange("p i n -> p (i n)"),
+            )
 
         steps = [
             (c, h)
@@ -164,8 +182,8 @@ def tile_multiheadattention_pa_t_kernel(tc, x, w, out):
                     out=xs_t[:, t, :],
                     lhsT=w_codes[:, h, cols].bitcast(FP8X4),
                     lhsT_scale=w_scales[:, h, cols],
-                    rhs=x_codes[c][:, rows].bitcast(FP8X4),
-                    rhs_scale=x_scales[c][:, rows],
+                    rhs=x_codes[c // PAIR][:, c % PAIR, rows].bitcast(FP8X4),
+                    rhs_scale=x_scales[c // PAIR][:, c % PAIR, rows],
                     start=True,
                     stop=True,
                 )
@@ -226,26 +244,26 @@ def tile_multiheadattention_pa_t_kernel(tc, x, w, out):
         keep_warm(4)
         transpose_x(0)
         keep_warm(3)
-        group_w(0, 0, nc.vector.tensor_copy)
-        group_w(0, 1, nc.scalar.copy)
-        quantise_x(0)
+        group_w(0, slice(0, 2), nc.vector.tensor_copy)
+        group_w(0, slice(2, 4), nc.scalar.copy)
+        quantise_x(0, 1)
         quantise_w(0, 0)
         transpose_x(1)
         keep_warm(1)
         quantise_w(0, 1)
-        quantise_x(1)
+        quantise_x(1, 1)
 
         runs = {0: range(2, GROUP)}
         for g in range(1, CHUNKS // GROUP):
             runs[2 + (g - 1) * RUN_STEPS] = range(g * GROUP, (g + 1) * GROUP)
 
+        for t in range(PACK):
+            group_w(1, slice(t, t + 1), gpsimd_copy)
+
         done = 0
         for s in range(STEPS):
             for c in runs.get(s, ()):
                 transpose_x(c)
-            if s == 1:
-                group_w(1, 0, nc.vector.tensor_copy)
-                group_w(1, 1, nc.scalar.copy)
             n = int(s >= LAG) + int(s == CATCH_UP)
             due = [(q, i) for q in range(done, done + n) for i in range(BLOCKS)]
             done += n
@@ -258,8 +276,10 @@ def tile_multiheadattention_pa_t_kernel(tc, x, w, out):
             if s == 2:
                 quantise_w(1, 0)
                 quantise_w(1, 1)
-            if s + 2 < STEPS and steps[s + 2][1] == 0:
-                quantise_x(steps[s + 2][0])
+            if s + 2 < STEPS:
+                c, h = steps[s + 2]
+                if h == 0 and c % PAIR == 0:
+                    quantise_x(c, PAIR)
         for q in range(done, STEPS):
             for i in range(BLOCKS):
                 second_product(q, i)

@@ -100,16 +100,6 @@ def tile_multiheadattention_pa_t_kernel(tc, x, w, out):
             grouped = keep.tile([P, PACK, P * PACK], BF16, tag="w_grouped%d" % h, align_bytes=64)
             w_grouped.append(grouped)
 
-        def gpsimd_copy(out, in_):
-            nc.gpsimd.tensor_scalar(
-                out=out,
-                in0=in_,
-                scalar1=1.0,
-                scalar2=0.0,
-                op0=mybir.AluOpType.mult,
-                op1=mybir.AluOpType.add,
-            )
-
         def group_w(h, blocks, copy):
             copy(
                 out=w_grouped[h][:, blocks, :].rearrange("p t (m k) -> p t m k", k=PACK),
@@ -257,13 +247,13 @@ def tile_multiheadattention_pa_t_kernel(tc, x, w, out):
         for g in range(1, CHUNKS // GROUP):
             runs[2 + (g - 1) * RUN_STEPS] = range(g * GROUP, (g + 1) * GROUP)
 
-        for t in range(PACK):
-            group_w(1, slice(t, t + 1), gpsimd_copy)
-
         done = 0
         for s in range(STEPS):
             for c in runs.get(s, ()):
                 transpose_x(c)
+            if s == 1:
+                group_w(1, slice(0, 2), nc.vector.tensor_copy)
+                group_w(1, slice(2, 4), nc.scalar.copy)
             n = int(s >= LAG) + int(s == CATCH_UP)
             due = [(q, i) for q in range(done, done + n) for i in range(BLOCKS)]
             done += n

from contextlib import ExitStack

import concourse.mybir as mybir
from concourse.masks import make_identity

BF16 = mybir.dt.bfloat16
F32 = mybir.dt.float32
U32 = mybir.dt.uint32
U8 = mybir.dt.uint8
FP8X4 = mybir.dt.float8_e4m3fn_x4

P = 128
PACK = 4
PSUM_BANKS = 8
PAIRS = 2
L, D, H = 4096, 512, 2
BLOCKS = 2
CHUNK = P * BLOCKS
CHUNKS = L // CHUNK
STEPS = CHUNKS * H
GROUP = 4
RUN_STEPS = GROUP * H
PAIR = 2
LAG = 4
CATCH_UP = STEPS - 4
X_TURNS = (4, (2, 3))
XS_TURNS = (4, (2,))
OUT_TURNS = (2, (0,))

FLOPS = 2 * H * 2 * L * D * D


def tile_multiheadattention_pa_t_kernel(tc, x, w, out):
    nc = tc.nc
    x_chunks = x[0].rearrange("(c p j) k -> c p (j k)", p=P, j=BLOCKS)
    out_chunks = out.rearrange("h (c p j) n -> h c p (j n)", p=P, j=BLOCKS)

    with ExitStack() as ctx:
        keep = ctx.enter_context(tc.tile_pool(name="keep", bufs=1))
        x_pool = ctx.enter_context(tc.tile_pool(name="x_rows", bufs=CHUNKS))
        x_stage = ctx.enter_context(tc.tile_pool(name="x_stage", bufs=CHUNKS // PAIR))
        x_grouped_pool = ctx.enter_context(tc.tile_pool(name="x_grouped", bufs=3))
        xs_stage = ctx.enter_context(tc.tile_pool(name="xs_stage", bufs=12))
        out_stage = ctx.enter_context(tc.tile_pool(name="out_stage", bufs=24))
        banks = ctx.enter_context(tc.psum_pool(name="banks", bufs=PSUM_BANKS))

        emptied = {X_TURNS: 0, XS_TURNS: 0, OUT_TURNS: 0}

        def empty_bank(dst, bank, turns):
            length, vector_turns = turns
            turn = emptied[turns] % length
            emptied[turns] += 1
            if turn in vector_turns:
                nc.vector.tensor_copy(out=dst, in_=bank)
            else:
                nc.scalar.copy(out=dst, in_=bank)

        x_rows = []
        w_rows = []

        def load_x(c):
            rows = x_pool.tile([P, BLOCKS * D], BF16, tag="x_rows")
            nc.sync.dma_start(out=rows[:], in_=x_chunks[c])
            x_rows.append(rows)

        def load_w(h):
            rows = keep.tile([P, PACK, D], BF16, tag="w_rows%d" % h)
            nc.sync.dma_start(
                out=rows[:].rearrange("p t n -> p (t n)"),
                in_=w[h].rearrange("(p t) n -> p (t n)", t=PACK),
            )
            w_rows.append(rows)

        load_x(0)
        load_w(0)
        for c in range(1, GROUP):
            load_x(c)
        load_w(1)
        for c in range(GROUP, CHUNKS):
            load_x(c)

        identity = keep.tile([P, P], F32)
        make_identity(nc, identity[:])

        zeros = keep.tile([P, D], BF16)
        nc.vector.memset(zeros[:], 0.0)
        unread = banks.tile([P, D], F32, tag="bank")

        def keep_warm(n):
            for i in range(n):
                nc.tensor.matmul(
                    out=unread[:], lhsT=zeros[:, :P], rhs=zeros[:], start=True, stop=True
                )

        w_codes = keep.tile([P, H, D], U32, align_bytes=64)
        w_scales = keep.tile([P, H, D], U8, align_bytes=64)
        w_grouped = []

        for h in range(H):
            grouped = keep.tile([P, PACK, P * PACK], BF16, tag="w_grouped%d" % h, align_bytes=64)
            w_grouped.append(grouped)

        def group_w(h, blocks, copy):
            copy(
                out=w_grouped[h][:, blocks, :].rearrange("p t (m k) -> p t m k", k=PACK),
                in_=w_rows[h][:].rearrange("p k (m t) -> p t m k", t=PACK)[:, blocks],
            )

        def quantise_w(h, half):
            cols = slice(half * D // 2, (half + 1) * D // 2)
            nc.vector.quantize_mx(
                out=w_codes[:, h, cols].bitcast(FP8X4),
                scales=w_scales[:, h, cols],
                in_=w_grouped[h][:, 2 * half : 2 * half + 2, :].rearrange("p t n -> p (t n)"),
            )

        x_grouped = {}
        x_codes = {}
        x_scales = {}

        def transpose_x(c):
            words = x_rows[c][:].bitcast(F32)
            pair, i = divmod(c, PAIR)
            if i == 0:
                grouped = x_grouped_pool.tile(
                    [P, PAIR, CHUNK * PACK], BF16, tag="x_grouped", align_bytes=64
                )
                codes = x_stage.tile([P, PAIR, CHUNK], U32, tag="x_codes", align_bytes=64)
                scales = x_stage.tile([P, PAIR, CHUNK], U8, tag="x_scales", align_bytes=64)
                x_grouped[pair], x_codes[pair], x_scales[pair] = grouped, codes, scales
            xt = banks.tile([P, PAIRS, CHUNK], F32, tag="bank")
            for j in range(BLOCKS):
                row = words[:, j * P * PAIRS : (j + 1) * P * PAIRS]
                for u in range(PAIRS):
                    nc.tensor.transpose(xt[:, u, j * P : (j + 1) * P], row[:, u::PAIRS], identity[:])
            empty_bank(
                x_grouped[pair][:, i, :].bitcast(F32).rearrange("p (r u) -> p r u", u=PAIRS),
                xt[:].rearrange("p u r -> p r u"),
                X_TURNS,
            )

        def quantise_x(first, n):
            pair, i = divmod(first, PAIR)
            chunks = slice(i, i + n)
            nc.vector.quantize_mx(
                out=x_codes[pair][:, chunks, :].rearrange("p i r -> p (i r)").bitcast(FP8X4),
                scales=x_scales[pair][:, chunks, :].rearrange("p i r -> p (i r)"),
                in_=x_grouped[pair][:, chunks, :].rearrange("p i n -> p (i n)"),
            )

        steps = [
            (c, h)
            for first in range(0, CHUNKS, GROUP)
            for h in range(H)
            for c in range(first, first + GROUP)
        ]

        xs_grouped = {}
        xs_codes = {}
        xs_scales = {}

        def first_product(s, j):
            c, h = steps[s]
            if j == 0:
                grouped = xs_stage.tile([P, CHUNK * PACK], BF16, tag="xs_grouped", align_bytes=64)
                xs_grouped[s] = grouped
            rows = slice(j * P, (j + 1) * P)
            xs_t = banks.tile([P, PACK, P], F32, tag="bank")
            for t in range(PACK):
                cols = slice(t * P, (t + 1) * P)
                nc.tensor.matmul_mx(
                    out=xs_t[:, t, :],
                    lhsT=w_codes[:, h, cols].bitcast(FP8X4),
                    lhsT_scale=w_scales[:, h, cols],
                    rhs=x_codes[c // PAIR][:, c % PAIR, rows].bitcast(FP8X4),
                    rhs_scale=x_scales[c // PAIR][:, c % PAIR, rows],
                    start=True,
                    stop=True,
                )
            empty_bank(
                xs_grouped[s][:, j * P * PACK : (j + 1) * P * PACK].rearrange(
                    "p (r t) -> p r t", t=PACK
                ),
                xs_t[:].rearrange("p t r -> p r t"),
                XS_TURNS,
            )

        def quantise_xs(s, rows=slice(0, CHUNK)):
            if rows.start == 0:
                codes = xs_stage.tile([P, CHUNK], U32, tag="xs_codes", align_bytes=64)
                scales = xs_stage.tile([P, CHUNK], U8, tag="xs_scales", align_bytes=64)
                xs_codes[s] = codes
                xs_scales[s] = scales
            nc.vector.quantize_mx(
                out=xs_codes[s][:, rows].bitcast(FP8X4),
                scales=xs_scales[s][:, rows],
                in_=xs_grouped[s][:, rows.start * PACK : rows.stop * PACK],
            )

        out_rows = {}

        def second_product(s, j):
            c, h = steps[s]
            if j == 0:
                result = out_stage.tile([P, BLOCKS, D], F32, tag="out_rows")
                out_rows[s] = result
            rows = slice(j * P, (j + 1) * P)
            acc = banks.tile([P, D], F32, tag="bank")
            nc.tensor.matmul_mx(
                out=acc[:],
                lhsT=xs_codes[s][:, rows].bitcast(FP8X4),
                lhsT_scale=xs_scales[s][:, rows],
                rhs=w_codes[:, h, :].bitcast(FP8X4),
                rhs_scale=w_scales[:, h, :],
                start=True,
                stop=True,
            )
            empty_bank(
                out_rows[s][:, j, :].rearrange("p (m t) -> p m t", t=PACK),
                acc[:].rearrange("p (t m) -> p m t", t=PACK),
                OUT_TURNS,
            )
            if s == STEPS - 1:
                nc.sync.dma_start(
                    out=out_chunks[h, c].rearrange("p (j n) -> p j n", j=BLOCKS)[:, j, :],
                    in_=out_rows[s][:, j, :],
                )
            elif j == BLOCKS - 1:
                nc.sync.dma_start(
                    out=out_chunks[h, c], in_=out_rows[s][:].rearrange("p j n -> p (j n)")
                )

        ctx.enter_context(tc.manual_schedule())
        keep_warm(4)
        transpose_x(0)
        keep_warm(3)
        group_w(0, slice(0, 2), nc.vector.tensor_copy)
        group_w(0, slice(2, 4), nc.scalar.copy)
        quantise_x(0, 1)
        quantise_w(0, 0)
        transpose_x(1)
        keep_warm(1)
        quantise_w(0, 1)
        quantise_x(1, 1)

        runs = {0: range(2, GROUP)}
        for g in range(1, CHUNKS // GROUP):
            runs[2 + (g - 1) * RUN_STEPS] = range(g * GROUP, (g + 1) * GROUP)

        done = 0
        for s in range(STEPS):
            for c in runs.get(s, ()):
                transpose_x(c)
            if s == 1:
                group_w(1, slice(0, 2), nc.vector.tensor_copy)
                group_w(1, slice(2, 4), nc.scalar.copy)
            n = int(s >= LAG) + int(s == CATCH_UP)
            due = [(q, i) for q in range(done, done + n) for i in range(BLOCKS)]
            done += n
            for j in range(BLOCKS):
                for q, i in due[j * n : (j + 1) * n]:
                    second_product(q, i)
                first_product(s, j)
                if j == 0 and s > 0:
                    quantise_xs(s - 1)
            if s == 2:
                quantise_w(1, 0)
                quantise_w(1, 1)
            if s + 2 < STEPS:
                c, h = steps[s + 2]
                if h == 0 and c % PAIR == 0:
                    quantise_x(c, PAIR)
        for q in range(done, STEPS):
            for i in range(BLOCKS):
                second_product(q, i)
                if q == done:
                    quantise_xs(STEPS - 1, slice(i * P, (i + 1) * P))
